import numpy as np
import ml_dtypes


def mxq(x, axis, fmt="e4m3"):
    dtype, down = {"e4m3": (ml_dtypes.float8_e4m3fn, 7), "e5m2": (ml_dtypes.float8_e5m2, 14)}[fmt]
    v = np.moveaxis(np.asarray(x, np.float32).astype(ml_dtypes.bfloat16).astype(np.float64), axis, -1)
    blocks = v.reshape(v.shape[:-1] + (-1, 32))
    amax = np.abs(blocks).max(-1, keepdims=True)
    byte = np.maximum(np.where(amax > 0, np.frexp(amax)[1] - 1 + 127, 0) - down, 1)
    scale = np.exp2(byte - 127.0)
    codes = (blocks / scale).astype(np.float32).astype(dtype).astype(np.float64)
    return np.moveaxis((codes * scale).reshape(v.shape), -1, axis)


WIDE = False


def mx_kscale(k):
    if not WIDE:
        return np.ones(k)
    levels = np.array([10, -10, 5, -5, 0])
    a = np.random.permutation(np.resize(levels, k // 512 * 4)).reshape(k // 512, 4)
    idx = np.arange(k)
    return np.exp2(a[idx // 512, idx % 128 // 32])


BF16 = ml_dtypes.bfloat16


def bf(x):
    return np.asarray(x, np.float32).astype(BF16)


def f64(x):
    return np.asarray(x).astype(np.float64)


T, K, N = 1024, 1024, 4096
KK_THRESHOLD = 1e6


def setup_inputs():
    s = mx_kscale(K)
    r = s / s.max()
    return {"inputs": bf(np.random.standard_normal((T, K)) * 4.0 / np.sqrt(K) / r),
            "weight": bf(np.random.uniform(-1.0, 1.0, (N, K)) * r),
            "bias": bf(np.random.standard_normal(N) * 0.5),
            "nmk": bf(1.0 + 0.1 * np.random.standard_normal(1)),
            "kk": bf(1.0 + 0.1 * np.random.standard_normal(1))}


def reference(inputs, weight, bias, nmk, kk):
    kk_s = f64(kk)[0]
    w = f64(weight)
    w_bin = np.where(kk_s < KK_THRESHOLD, np.tanh(w * kk_s), np.sign(w))
    out = (mxq(f64(inputs), 1, "e4m3") @ mxq(w_bin, 1, "e4m3").T) + f64(bias)
    return f64(nmk)[0] * out

@@ -1,0 +1,174 @@
+from contextlib import ExitStack
+
+import concourse.bass as bass
+import concourse.mybir as mybir
+import concourse.tile as tile
+from concourse.masks import make_identity
+
+F32 = mybir.dt.float32
+BF16 = mybir.dt.bfloat16
+U32 = mybir.dt.uint32
+U8 = mybir.dt.uint8
+I32 = mybir.dt.int32
+FP8X4 = mybir.dt.float8_e4m3fn_x4
+ACT = mybir.ActivationFunctionType
+ALU = mybir.AluOpType
+
+P = 128
+T, K, N = 1024, 1024, 4096
+FLOPS = 2 * T * K * N
+NA = T // P
+CH = 512
+NCH = N // CH
+G = K // 512
+BIG = 3.4e38
+KK_THRESHOLD = 1.0e6
+PIN = False
+A_ST = 2
+
+
+def tile_binarydense_kernel(tc, inputs, weight, bias, nmk, kk, out):
+    nc = tc.nc
+    with ExitStack() as ctx:
+        const = ctx.enter_context(tc.tile_pool(name="const", bufs=1))
+        wgp = ctx.enter_context(tc.tile_pool(name="wgp", bufs=2))
+        wcp = ctx.enter_context(tc.tile_pool(name="wcp", bufs=3))
+        osp = ctx.enter_context(tc.tile_pool(name="osp", bufs=12))
+        ps_t = ctx.enter_context(tc.psum_pool(name="ps_t", bufs=4))
+        ps_a = ctx.enter_context(tc.psum_pool(name="ps_a", bufs=4))
+        if PIN:
+            ctx.enter_context(tc.manual_schedule())
+
+        kk_bf = const.tile([P, 1], BF16, name="kk_bf")
+        nc.sync.dma_start(out=kk_bf[:], in_=kk.partition_broadcast(P))
+        nmk_bf = const.tile([P, 1], BF16, name="nmk_bf")
+        nc.scalar.dma_start(out=nmk_bf[:], in_=nmk.partition_broadcast(P))
+        brow = const.tile([P, CH], BF16, name="brow")
+        nc.vector.memset(brow[:].bitcast(I32), 0)
+        nc.scalar.dma_start(out=brow[0:NCH, :], in_=bias.rearrange("(c j) -> c j", c=NCH))
+
+        w_raw = []
+        for c in range(NCH):
+            w_raw.append(const.tile([P, 4 * K], BF16, name="w_raw%d" % c))
+        x_raw = const.tile([P, NA * K], BF16, name="x_raw")
+
+        def load_w(c, parts):
+            src = weight[c * CH:(c + 1) * CH, :].rearrange("(p b) k -> p (b k)", b=4)
+            w = 4 * K // parts
+            for i in range(parts):
+                nc.sync.dma_start(out=w_raw[c][:, i * w:(i + 1) * w], in_=src[:, i * w:(i + 1) * w])
+
+        load_w(0, 2)
+        x_src = inputs.rearrange("(p a) k -> p (a k)", a=NA)
+        for i in range(4):
+            nc.sync.dma_start(out=x_raw[:, i * 2048:(i + 1) * 2048], in_=x_src[:, i * 2048:(i + 1) * 2048])
+        for c in range(1, NCH):
+            load_w(c, 1)
+
+        ident_f = const.tile([P, P], F32, name="ident_f")
+        make_identity(nc, ident_f[:])
+        ident_b = const.tile([P, P], BF16, name="ident_b")
+        make_identity(nc, ident_b[:])
+        kk_m = const.tile([P, 1], F32, name="kk_m")
+        nc.vector.tensor_scalar(out=kk_m[:], in0=kk_bf[:], scalar1=KK_THRESHOLD, scalar2=BIG,
+                                op0=ALU.is_ge, op1=ALU.mult)
+        kk_eff = const.tile([P, 1], F32, name="kk_eff")
+        nc.vector.tensor_scalar(out=kk_eff[:], in0=kk_bf[:], scalar1=kk_m[:, 0:1], scalar2=BIG,
+                                op0=ALU.add, op1=ALU.min)
+        nmk_f = const.tile([P, 1], F32, name="nmk_f")
+        nc.vector.tensor_copy(out=nmk_f[:], in_=nmk_bf[:])
+
+        bias_n = const.tile([P, N], F32, name="bias_n")
+        xg = const.tile([P, G, NA * 512], BF16, name="xg", align_bytes=64)
+        xc = const.tile([P, G, T], U32, name="xc", align_bytes=64)
+        xs = const.tile([P, G, T], U8, name="xs", align_bytes=64)
+        xgf = xg[:].bitcast(F32)
+        xf = x_raw[:].bitcast(F32)
+        out_v = out.rearrange("(r a) n -> r a n", a=NA)
+
+        wg_t = {}
+        wc_t = {}
+        ws_t = {}
+
+        def bias_chunk(c):
+            bp = ps_t.tile([P, CH], F32, name="bp", tag="tp")
+            nc.tensor.matmul(out=bp[:], lhsT=ident_b[:, c:c + 1].to_broadcast([P, P]), rhs=brow[:],
+                             start=True, stop=True)
+            nc.scalar.activation(out=bias_n[:, c * CH:(c + 1) * CH], in_=bp[:], func=ACT.Copy,
+                                 scale=nmk_f[:, 0:1])
+
+        def w_transpose(c):
+            wf = w_raw[c][:].bitcast(F32)
+            wg = wgp.tile([P, G, 4 * CH], BF16, name="wg", align_bytes=64)
+            wg_t[c] = wg
+            order = [(g, bh) for bh in range(2) for g in range(G)] if c == 0 else \
+                    [(g, bh) for g in range(G) for bh in range(2)]
+            for g, bh in order:
+                tp = ps_t.tile([P, 512], F32, name="tp", tag="tp")
+                for m in range(4):
+                    b = 2 * bh + m // 2
+                    u = m % 2
+                    col = 512 * b + 256 * g + 128 * u
+                    nc.tensor.transpose(tp[:, 128 * m:128 * m + 128], wf[:, col:col + 128], ident_f[:])
+                src = tp[:].bitcast(BF16).rearrange("p (m n e) -> p n m e", m=4, n=P, e=2)
+                dst = wg[:, g, :].rearrange("p (n h m e) -> p n h m e", n=P, h=2, m=4, e=2)[:, :, bh, :, :]
+                nc.scalar.activation(out=dst, in_=src, func=ACT.Tanh, scale=kk_eff[:, 0:1])
+
+        def w_quant(c):
+            wc = wcp.tile([P, G, CH], U32, name="wc", align_bytes=64)
+            ws = wcp.tile([P, G, CH], U8, name="ws", align_bytes=64)
+            wc_t[c] = wc
+            ws_t[c] = ws
+            for g in range(G):
+                nc.vector.quantize_mx(out=wc[:, g, :].bitcast(FP8X4), scales=ws[:, g, :], in_=wg_t[c][:, g, :])
+
+        def x_transpose(a):
+            tpx = ps_a.tile([P, 512], F32, name="tpx", tag="acc")
+            for j in range(4):
+                col = 512 * a + 128 * j
+                nc.tensor.transpose(tpx[:, 128 * j:128 * j + 128], xf[:, col:col + 128], ident_f[:])
+            nc.vector.tensor_copy(
+                out=xgf[:, :, 256 * a:256 * a + 256].rearrange("p g (r u) -> p g r u", u=2),
+                in_=tpx[:].rearrange("p (g u r) -> p g r u", g=G, u=2))
+
+        def x_quant(q):
+            for g in range(G):
+                nc.vector.quantize_mx(out=xc[:, g, 512 * q:512 * q + 512].bitcast(FP8X4),
+                                      scales=xs[:, g, 512 * q:512 * q + 512],
+                                      in_=xg[:, g, 2048 * q:2048 * q + 2048])
+
+        def mx_chunk(c):
+            wc = wc_t[c]
+            ws = ws_t[c]
+            ost = None
+            for a in range(NA):
+                acc = ps_a.tile([P, CH], F32, name="acc", tag="acc")
+                for g in range(G):
+                    nc.tensor.matmul_mx(out=acc[:],
+                                        lhsT=xc[:, g, P * a:P * a + P].bitcast(FP8X4),
+                                        lhsT_scale=xs[:, g, P * a:P * a + P],
+                                        rhs=wc[:, g, :].bitcast(FP8X4),
+                                        rhs_scale=ws[:, g, :],
+                                        start=(g == 0), stop=(g == G - 1))
+                if a % A_ST == 0:
+                    ost = osp.tile([P, A_ST, CH], F32, name="ost")
+                nc.vector.scalar_tensor_tensor(out=ost[:, a % A_ST, :], in0=acc[:], scalar=nmk_f[:, 0:1],
+                                               in1=bias_n[:, c * CH:(c + 1) * CH],
+                                               op0=ALU.mult, op1=ALU.add)
+                if a % A_ST == A_ST - 1:
+                    nc.sync.dma_start(out=out_v[:, a - A_ST + 1:a + 1, c * CH:(c + 1) * CH], in_=ost[:])
+
+        w_transpose(0)
+        for a in range(NA):
+            x_transpose(a)
+            if a % 4 == 3:
+                x_quant(a // 4)
+        bias_chunk(0)
+        w_quant(0)
+        for c in range(NCH):
+            if c + 1 < NCH:
+                bias_chunk(c + 1)
+                w_transpose(c + 1)
+            mx_chunk(c)
+            if c + 1 < NCH:
+                w_quant(c + 1)

@@ -1,8 +1,6 @@
 from contextlib import ExitStack
 
-import concourse.bass as bass
 import concourse.mybir as mybir
-import concourse.tile as tile
 from concourse.masks import make_identity
 
 F32 = mybir.dt.float32
@@ -23,8 +21,12 @@ NCH = N // CH
 G = K // 512
 BIG = 3.4e38
 KK_THRESHOLD = 1.0e6
-PIN = False
+PIN = True
 A_ST = 2
+OFFLOAD = []
+QH = (2, 5)
+QH0 = (5, 7)
+T1_AFTER = 1
 
 
 def tile_binarydense_kernel(tc, inputs, weight, bias, nmk, kk, out):
@@ -51,19 +53,24 @@ def tile_binarydense_kernel(tc, inputs, weight, bias, nmk, kk, out):
         for c in range(NCH):
             w_raw.append(const.tile([P, 4 * K], BF16, name="w_raw%d" % c))
         x_raw = const.tile([P, NA * K], BF16, name="x_raw")
+        x_src = inputs.rearrange("(p a) k -> p (a k)", a=NA)
 
-        def load_w(c, parts):
+        def load_w(c, i, parts):
             src = weight[c * CH:(c + 1) * CH, :].rearrange("(p b) k -> p (b k)", b=4)
             w = 4 * K // parts
-            for i in range(parts):
-                nc.sync.dma_start(out=w_raw[c][:, i * w:(i + 1) * w], in_=src[:, i * w:(i + 1) * w])
+            nc.sync.dma_start(out=w_raw[c][:, i * w:(i + 1) * w], in_=src[:, i * w:(i + 1) * w])
 
-        load_w(0, 2)
-        x_src = inputs.rearrange("(p a) k -> p (a k)", a=NA)
-        for i in range(4):
+        def load_x(i):
             nc.sync.dma_start(out=x_raw[:, i * 2048:(i + 1) * 2048], in_=x_src[:, i * 2048:(i + 1) * 2048])
+
+        load_w(0, 0, 2)
+        load_x(0)
+        load_w(0, 1, 2)
+        load_x(1)
+        load_x(2)
+        load_x(3)
         for c in range(1, NCH):
-            load_w(c, 1)
+            load_w(c, 0, 1)
 
         ident_f = const.tile([P, P], F32, name="ident_f")
         make_identity(nc, ident_f[:])
@@ -97,50 +104,57 @@ def tile_binarydense_kernel(tc, inputs, weight, bias, nmk, kk, out):
             nc.scalar.activation(out=bias_n[:, c * CH:(c + 1) * CH], in_=bp[:], func=ACT.Copy,
                                  scale=nmk_f[:, 0:1])
 
-        def w_transpose(c):
+        def w_bank(c, g, bh):
             wf = w_raw[c][:].bitcast(F32)
-            wg = wgp.tile([P, G, 4 * CH], BF16, name="wg", align_bytes=64)
-            wg_t[c] = wg
-            order = [(g, bh) for bh in range(2) for g in range(G)] if c == 0 else \
-                    [(g, bh) for g in range(G) for bh in range(2)]
-            for g, bh in order:
-                tp = ps_t.tile([P, 512], F32, name="tp", tag="tp")
-                for m in range(4):
-                    b = 2 * bh + m // 2
-                    u = m % 2
-                    col = 512 * b + 256 * g + 128 * u
-                    nc.tensor.transpose(tp[:, 128 * m:128 * m + 128], wf[:, col:col + 128], ident_f[:])
-                src = tp[:].bitcast(BF16).rearrange("p (m n e) -> p n m e", m=4, n=P, e=2)
-                dst = wg[:, g, :].rearrange("p (n h m e) -> p n h m e", n=P, h=2, m=4, e=2)[:, :, bh, :, :]
-                nc.scalar.activation(out=dst, in_=src, func=ACT.Tanh, scale=kk_eff[:, 0:1])
+            wg = wg_t[c]
+            tp = ps_t.tile([P, 512], F32, name="tp", tag="tp")
+            for m in range(4):
+                col = 512 * (2 * bh + m // 2) + 256 * g + 128 * (m % 2)
+                nc.tensor.transpose(tp[:, 128 * m:128 * m + 128], wf[:, col:col + 128], ident_f[:])
+            src = tp[:].bitcast(BF16).rearrange("p (m n e) -> p n m e", m=4, n=P, e=2)
+            dst = wg[:, g, :].rearrange("p (n h m e) -> p n h m e", n=P, h=2, m=4, e=2)[:, :, bh, :, :]
+            nc.scalar.activation(out=dst, in_=src, func=ACT.Tanh, scale=kk_eff[:, 0:1])
 
-        def w_quant(c):
-            wc = wcp.tile([P, G, CH], U32, name="wc", align_bytes=64)
-            ws = wcp.tile([P, G, CH], U8, name="ws", align_bytes=64)
-            wc_t[c] = wc
-            ws_t[c] = ws
+        def w_new(c):
+            wg_t[c] = wgp.tile([P, G, 4 * CH], BF16, name="wg", align_bytes=64)
+
+        def w_transpose(c):
+            w_new(c)
             for g in range(G):
-                nc.vector.quantize_mx(out=wc[:, g, :].bitcast(FP8X4), scales=ws[:, g, :], in_=wg_t[c][:, g, :])
+                for bh in range(2):
+                    w_bank(c, g, bh)
 
-        def x_transpose(a):
+        def w_quant(c, g):
+            if g == 0:
+                wc_t[c] = wcp.tile([P, G, CH], U32, name="wc", align_bytes=64)
+                ws_t[c] = wcp.tile([P, G, CH], U8, name="ws", align_bytes=64)
+            nc.vector.quantize_mx(out=wc_t[c][:, g, :].bitcast(FP8X4), scales=ws_t[c][:, g, :],
+                                  in_=wg_t[c][:, g, :])
+
+        def x_transpose(a, eng):
             tpx = ps_a.tile([P, 512], F32, name="tpx", tag="acc")
             for j in range(4):
                 col = 512 * a + 128 * j
                 nc.tensor.transpose(tpx[:, 128 * j:128 * j + 128], xf[:, col:col + 128], ident_f[:])
-            nc.vector.tensor_copy(
-                out=xgf[:, :, 256 * a:256 * a + 256].rearrange("p g (r u) -> p g r u", u=2),
-                in_=tpx[:].rearrange("p (g u r) -> p g r u", g=G, u=2))
+            dst = xgf[:, :, 256 * a:256 * a + 256].rearrange("p g (r u) -> p g r u", u=2)
+            src = tpx[:].rearrange("p (g u r) -> p g r u", g=G, u=2)
+            if eng == "v":
+                nc.vector.tensor_copy(out=dst, in_=src)
+            else:
+                nc.scalar.copy(out=dst, in_=src)
 
         def x_quant(q):
             for g in range(G):
-                nc.vector.quantize_mx(out=xc[:, g, 512 * q:512 * q + 512].bitcast(FP8X4),
-                                      scales=xs[:, g, 512 * q:512 * q + 512],
-                                      in_=xg[:, g, 2048 * q:2048 * q + 2048])
+                nc.vector.quantize_mx(out=xc[:, g, 256 * q:256 * q + 256].bitcast(FP8X4),
+                                      scales=xs[:, g, 256 * q:256 * q + 256],
+                                      in_=xg[:, g, 1024 * q:1024 * q + 1024])
 
-        def mx_chunk(c):
+        ost_t = {}
+
+        def mx_chunk(c, t_hooks, v_hooks):
             wc = wc_t[c]
             ws = ws_t[c]
-            ost = None
+            cs = slice(c * CH, (c + 1) * CH)
             for a in range(NA):
                 acc = ps_a.tile([P, CH], F32, name="acc", tag="acc")
                 for g in range(G):
@@ -150,25 +164,57 @@ def tile_binarydense_kernel(tc, inputs, weight, bias, nmk, kk, out):
                                         rhs=wc[:, g, :].bitcast(FP8X4),
                                         rhs_scale=ws[:, g, :],
                                         start=(g == 0), stop=(g == G - 1))
+                for f in t_hooks.get(a, []):
+                    f()
                 if a % A_ST == 0:
-                    ost = osp.tile([P, A_ST, CH], F32, name="ost")
-                nc.vector.scalar_tensor_tensor(out=ost[:, a % A_ST, :], in0=acc[:], scalar=nmk_f[:, 0:1],
-                                               in1=bias_n[:, c * CH:(c + 1) * CH],
-                                               op0=ALU.mult, op1=ALU.add)
+                    ost_t[0] = osp.tile([P, A_ST, CH], F32, name="ost")
+                ost = ost_t[0]
+                if a in OFFLOAD:
+                    nc.scalar.activation(out=ost[:, a % A_ST, :], in_=acc[:], func=ACT.Copy,
+                                         scale=nmk_f[:, 0:1])
+                    nc.gpsimd.tensor_tensor(out=ost[:, a % A_ST, :], in0=ost[:, a % A_ST, :],
+                                            in1=bias_n[:, cs], op=ALU.add)
+                else:
+                    nc.vector.scalar_tensor_tensor(out=ost[:, a % A_ST, :], in0=acc[:], scalar=nmk_f[:, 0:1],
+                                                   in1=bias_n[:, cs], op0=ALU.mult, op1=ALU.add)
                 if a % A_ST == A_ST - 1:
-                    nc.sync.dma_start(out=out_v[:, a - A_ST + 1:a + 1, c * CH:(c + 1) * CH], in_=ost[:])
+                    nc.sync.dma_start(out=out_v[:, a - A_ST + 1:a + 1, cs], in_=ost[:])
+                for f in v_hooks.get(a, []):
+                    f()
 
-        w_transpose(0)
-        for a in range(NA):
-            x_transpose(a)
-            if a % 4 == 3:
-                x_quant(a // 4)
+        w_new(0)
+        w_bank(0, 0, 0)
+        w_bank(0, 1, 0)
+        x_transpose(0, "v")
+        x_transpose(1, "v")
+        x_quant(0)
+        w_bank(0, 0, 1)
+        w_bank(0, 1, 1)
         bias_chunk(0)
-        w_quant(0)
+        x_transpose(2, "v")
+        x_transpose(3, "v")
+        x_quant(1)
+        for a in range(4, NA):
+            x_transpose(a, "s")
+        w_quant(0, 0)
+        w_quant(0, 1)
+        x_quant(2)
+
+        def t_run(c):
+            bias_chunk(c)
+            w_transpose(c)
+
         for c in range(NCH):
-            if c + 1 < NCH:
-                bias_chunk(c + 1)
-                w_transpose(c + 1)
-            mx_chunk(c)
-            if c + 1 < NCH:
-                w_quant(c + 1)
+            t_hooks = {}
+            v_hooks = {}
+            if c == 0:
+                t_hooks[T1_AFTER] = [lambda: t_run(1)]
+                v_hooks[0] = [lambda: x_quant(3)]
+                v_hooks[QH0[0]] = [lambda: w_quant(1, 0)]
+                v_hooks[QH0[1]] = [lambda: w_quant(1, 1)]
+            elif c + 1 < NCH:
+                n = c + 1
+                v_hooks[QH[0]] = [lambda: w_quant(n, 0)]
+                v_hooks[QH[1]] = [lambda: w_quant(n, 1)]
+                t_run(n)
+            mx_chunk(c, t_hooks, v_hooks)

@@ -27,6 +27,7 @@ OFFLOAD = []
 QH = (2, 5)
 QH0 = (5, 7)
 T1_AFTER = 1
+NPAIR = 3
 
 
 def tile_binarydense_kernel(tc, inputs, weight, bias, nmk, kk, out):
@@ -35,7 +36,8 @@ def tile_binarydense_kernel(tc, inputs, weight, bias, nmk, kk, out):
         const = ctx.enter_context(tc.tile_pool(name="const", bufs=1))
         wgp = ctx.enter_context(tc.tile_pool(name="wgp", bufs=2))
         wcp = ctx.enter_context(tc.tile_pool(name="wcp", bufs=3))
-        osp = ctx.enter_context(tc.tile_pool(name="osp", bufs=12))
+        osp = ctx.enter_context(tc.tile_pool(name="osp", bufs=6))
+        wrp = ctx.enter_context(tc.tile_pool(name="wrp", bufs=6))
         ps_t = ctx.enter_context(tc.psum_pool(name="ps_t", bufs=4))
         ps_a = ctx.enter_context(tc.psum_pool(name="ps_a", bufs=4))
         if PIN:
@@ -49,15 +51,15 @@ def tile_binarydense_kernel(tc, inputs, weight, bias, nmk, kk, out):
         nc.vector.memset(brow[:].bitcast(I32), 0)
         nc.scalar.dma_start(out=brow[0:NCH, :], in_=bias.rearrange("(c j) -> c j", c=NCH))
 
-        w_raw = []
-        for c in range(NCH):
-            w_raw.append(const.tile([P, 4 * K], BF16, name="w_raw%d" % c))
-        x_raw = const.tile([P, NA * K], BF16, name="x_raw")
+        w_raw = {}
+        x_raw = osp.tile([P, NA * K], BF16, name="x_raw", tag="ost", align_bytes=64)
         x_src = inputs.rearrange("(p a) k -> p (a k)", a=NA)
 
         def load_w(c, i, parts):
             src = weight[c * CH:(c + 1) * CH, :].rearrange("(p b) k -> p (b k)", b=4)
             w = 4 * K // parts
+            if i == 0:
+                w_raw[c] = wrp.tile([P, 4 * K], BF16, name="w_raw")
             nc.sync.dma_start(out=w_raw[c][:, i * w:(i + 1) * w], in_=src[:, i * w:(i + 1) * w])
 
         def load_x(i):
@@ -69,7 +71,7 @@ def tile_binarydense_kernel(tc, inputs, weight, bias, nmk, kk, out):
         load_x(1)
         load_x(2)
         load_x(3)
-        for c in range(1, NCH):
+        for c in range(1, 6):
             load_w(c, 0, 1)
 
         ident_f = const.tile([P, P], F32, name="ident_f")
@@ -86,7 +88,7 @@ def tile_binarydense_kernel(tc, inputs, weight, bias, nmk, kk, out):
         nc.vector.tensor_copy(out=nmk_f[:], in_=nmk_bf[:])
 
         bias_n = const.tile([P, N], F32, name="bias_n")
-        xg = const.tile([P, G, NA * 512], BF16, name="xg", align_bytes=64)
+        xg = osp.tile([P, G, NA * 512], BF16, name="xg", tag="ost", align_bytes=64)
         xc = const.tile([P, G, T], U32, name="xc", align_bytes=64)
         xs = const.tile([P, G, T], U8, name="xs", align_bytes=64)
         xgf = xg[:].bitcast(F32)
@@ -166,19 +168,25 @@ def tile_binarydense_kernel(tc, inputs, weight, bias, nmk, kk, out):
                                         start=(g == 0), stop=(g == G - 1))
                 for f in t_hooks.get(a, []):
                     f()
-                if a % A_ST == 0:
-                    ost_t[0] = osp.tile([P, A_ST, CH], F32, name="ost")
-                ost = ost_t[0]
+                paired = c < 2 * NPAIR
+                width = 2 * CH if paired else CH
+                if a % 4 == 0 and not (paired and c % 2 == 1):
+                    ost_t[a // 4] = osp.tile([P, 4, width], F32, name="ost", tag="ost", align_bytes=64)
+                off = CH if (paired and c % 2 == 1) else 0
+                ost = ost_t[a // 4][:, :, off:off + CH]
+                a4 = a % 4
                 if a in OFFLOAD:
-                    nc.scalar.activation(out=ost[:, a % A_ST, :], in_=acc[:], func=ACT.Copy,
+                    nc.scalar.activation(out=ost[:, a4, :], in_=acc[:], func=ACT.Copy,
                                          scale=nmk_f[:, 0:1])
-                    nc.gpsimd.tensor_tensor(out=ost[:, a % A_ST, :], in0=ost[:, a % A_ST, :],
+                    nc.gpsimd.tensor_tensor(out=ost[:, a4, :], in0=ost[:, a4, :],
                                             in1=bias_n[:, cs], op=ALU.add)
                 else:
-                    nc.vector.scalar_tensor_tensor(out=ost[:, a % A_ST, :], in0=acc[:], scalar=nmk_f[:, 0:1],
+                    nc.vector.scalar_tensor_tensor(out=ost[:, a4, :], in0=acc[:], scalar=nmk_f[:, 0:1],
                                                    in1=bias_n[:, cs], op0=ALU.mult, op1=ALU.add)
-                if a % A_ST == A_ST - 1:
-                    nc.sync.dma_start(out=out_v[:, a - A_ST + 1:a + 1, cs], in_=ost[:])
+                if a % A_ST == A_ST - 1 and not (paired and c % 2 == 0):
+                    lo = (c - 1) * CH if paired else c * CH
+                    nc.sync.dma_start(out=out_v[:, a - A_ST + 1:a + 1, lo:(c + 1) * CH],
+                                      in_=ost_t[a // 4][:, a4 - A_ST + 1:a4 + 1, :])
                 for f in v_hooks.get(a, []):
                     f()
 
@@ -190,6 +198,7 @@ def tile_binarydense_kernel(tc, inputs, weight, bias, nmk, kk, out):
         x_quant(0)
         w_bank(0, 0, 1)
         w_bank(0, 1, 1)
+        load_w(6, 0, 1)
         bias_chunk(0)
         x_transpose(2, "v")
         x_transpose(3, "v")
@@ -208,7 +217,7 @@ def tile_binarydense_kernel(tc, inputs, weight, bias, nmk, kk, out):
             t_hooks = {}
             v_hooks = {}
             if c == 0:
-                t_hooks[T1_AFTER] = [lambda: t_run(1)]
+                t_hooks[T1_AFTER] = [lambda: t_run(1), lambda: load_w(7, 0, 1)]
                 v_hooks[0] = [lambda: x_quant(3)]
                 v_hooks[QH0[0]] = [lambda: w_quant(1, 0)]
                 v_hooks[QH0[1]] = [lambda: w_quant(1, 1)]

@@ -23,11 +23,10 @@ BIG = 3.4e38
 KK_THRESHOLD = 1.0e6
 PIN = True
 A_ST = 2
-OFFLOAD = []
+OFFLOAD = [7]
 QH = (2, 5)
 QH0 = (5, 7)
 T1_AFTER = 1
-NPAIR = 3
 
 
 def tile_binarydense_kernel(tc, inputs, weight, bias, nmk, kk, out):
@@ -36,8 +35,7 @@ def tile_binarydense_kernel(tc, inputs, weight, bias, nmk, kk, out):
         const = ctx.enter_context(tc.tile_pool(name="const", bufs=1))
         wgp = ctx.enter_context(tc.tile_pool(name="wgp", bufs=2))
         wcp = ctx.enter_context(tc.tile_pool(name="wcp", bufs=3))
-        osp = ctx.enter_context(tc.tile_pool(name="osp", bufs=6))
-        wrp = ctx.enter_context(tc.tile_pool(name="wrp", bufs=6))
+        osp = ctx.enter_context(tc.tile_pool(name="osp", bufs=12))
         ps_t = ctx.enter_context(tc.psum_pool(name="ps_t", bufs=4))
         ps_a = ctx.enter_context(tc.psum_pool(name="ps_a", bufs=4))
         if PIN:
@@ -51,15 +49,15 @@ def tile_binarydense_kernel(tc, inputs, weight, bias, nmk, kk, out):
         nc.vector.memset(brow[:].bitcast(I32), 0)
         nc.scalar.dma_start(out=brow[0:NCH, :], in_=bias.rearrange("(c j) -> c j", c=NCH))
 
-        w_raw = {}
-        x_raw = osp.tile([P, NA * K], BF16, name="x_raw", tag="ost", align_bytes=64)
+        w_raw = []
+        for c in range(NCH):
+            w_raw.append(const.tile([P, 4 * K], BF16, name="w_raw%d" % c))
+        x_raw = const.tile([P, NA * K], BF16, name="x_raw")
         x_src = inputs.rearrange("(p a) k -> p (a k)", a=NA)
 
         def load_w(c, i, parts):
             src = weight[c * CH:(c + 1) * CH, :].rearrange("(p b) k -> p (b k)", b=4)
             w = 4 * K // parts
-            if i == 0:
-                w_raw[c] = wrp.tile([P, 4 * K], BF16, name="w_raw")
             nc.sync.dma_start(out=w_raw[c][:, i * w:(i + 1) * w], in_=src[:, i * w:(i + 1) * w])
 
         def load_x(i):
@@ -71,7 +69,7 @@ def tile_binarydense_kernel(tc, inputs, weight, bias, nmk, kk, out):
         load_x(1)
         load_x(2)
         load_x(3)
-        for c in range(1, 6):
+        for c in range(1, NCH):
             load_w(c, 0, 1)
 
         ident_f = const.tile([P, P], F32, name="ident_f")
@@ -88,7 +86,7 @@ def tile_binarydense_kernel(tc, inputs, weight, bias, nmk, kk, out):
         nc.vector.tensor_copy(out=nmk_f[:], in_=nmk_bf[:])
 
         bias_n = const.tile([P, N], F32, name="bias_n")
-        xg = osp.tile([P, G, NA * 512], BF16, name="xg", tag="ost", align_bytes=64)
+        xg = const.tile([P, G, NA * 512], BF16, name="xg", align_bytes=64)
         xc = const.tile([P, G, T], U32, name="xc", align_bytes=64)
         xs = const.tile([P, G, T], U8, name="xs", align_bytes=64)
         xgf = xg[:].bitcast(F32)
@@ -168,25 +166,19 @@ def tile_binarydense_kernel(tc, inputs, weight, bias, nmk, kk, out):
                                         start=(g == 0), stop=(g == G - 1))
                 for f in t_hooks.get(a, []):
                     f()
-                paired = c < 2 * NPAIR
-                width = 2 * CH if paired else CH
-                if a % 4 == 0 and not (paired and c % 2 == 1):
-                    ost_t[a // 4] = osp.tile([P, 4, width], F32, name="ost", tag="ost", align_bytes=64)
-                off = CH if (paired and c % 2 == 1) else 0
-                ost = ost_t[a // 4][:, :, off:off + CH]
-                a4 = a % 4
-                if a in OFFLOAD:
-                    nc.scalar.activation(out=ost[:, a4, :], in_=acc[:], func=ACT.Copy,
+                if a % A_ST == 0:
+                    ost_t[0] = osp.tile([P, A_ST, CH], F32, name="ost")
+                ost = ost_t[0]
+                if a in OFFLOAD and c < NCH - 1:
+                    nc.scalar.activation(out=ost[:, a % A_ST, :], in_=acc[:], func=ACT.Copy,
                                          scale=nmk_f[:, 0:1])
-                    nc.gpsimd.tensor_tensor(out=ost[:, a4, :], in0=ost[:, a4, :],
+                    nc.gpsimd.tensor_tensor(out=ost[:, a % A_ST, :], in0=ost[:, a % A_ST, :],
                                             in1=bias_n[:, cs], op=ALU.add)
                 else:
-                    nc.vector.scalar_tensor_tensor(out=ost[:, a4, :], in0=acc[:], scalar=nmk_f[:, 0:1],
+                    nc.vector.scalar_tensor_tensor(out=ost[:, a % A_ST, :], in0=acc[:], scalar=nmk_f[:, 0:1],
                                                    in1=bias_n[:, cs], op0=ALU.mult, op1=ALU.add)
-                if a % A_ST == A_ST - 1 and not (paired and c % 2 == 0):
-                    lo = (c - 1) * CH if paired else c * CH
-                    nc.sync.dma_start(out=out_v[:, a - A_ST + 1:a + 1, lo:(c + 1) * CH],
-                                      in_=ost_t[a // 4][:, a4 - A_ST + 1:a4 + 1, :])
+                if a % A_ST == A_ST - 1:
+                    nc.sync.dma_start(out=out_v[:, a - A_ST + 1:a + 1, cs], in_=ost[:])
                 for f in v_hooks.get(a, []):
                     f()
 
@@ -198,7 +190,6 @@ def tile_binarydense_kernel(tc, inputs, weight, bias, nmk, kk, out):
         x_quant(0)
         w_bank(0, 0, 1)
         w_bank(0, 1, 1)
-        load_w(6, 0, 1)
         bias_chunk(0)
         x_transpose(2, "v")
         x_transpose(3, "v")
@@ -217,7 +208,7 @@ def tile_binarydense_kernel(tc, inputs, weight, bias, nmk, kk, out):
             t_hooks = {}
             v_hooks = {}
             if c == 0:
-                t_hooks[T1_AFTER] = [lambda: t_run(1), lambda: load_w(7, 0, 1)]
+                t_hooks[T1_AFTER] = [lambda: t_run(1)]
                 v_hooks[0] = [lambda: x_quant(3)]
                 v_hooks[QH0[0]] = [lambda: w_quant(1, 0)]
                 v_hooks[QH0[1]] = [lambda: w_quant(1, 1)]

@@ -23,7 +23,7 @@ BIG = 3.4e38
 KK_THRESHOLD = 1.0e6
 PIN = True
 A_ST = 2
-OFFLOAD = [7]
+OFFLOAD = []
 QH = (2, 5)
 QH0 = (5, 7)
 T1_AFTER = 1
@@ -56,9 +56,10 @@ def tile_binarydense_kernel(tc, inputs, weight, bias, nmk, kk, out):
         x_src = inputs.rearrange("(p a) k -> p (a k)", a=NA)
 
         def load_w(c, i, parts):
-            src = weight[c * CH:(c + 1) * CH, :].rearrange("(p b) k -> p (b k)", b=4)
-            w = 4 * K // parts
-            nc.sync.dma_start(out=w_raw[c][:, i * w:(i + 1) * w], in_=src[:, i * w:(i + 1) * w])
+            src = weight[c * CH:(c + 1) * CH, :].rearrange("(b p) k -> p b k", p=P)
+            nb = 4 // parts
+            nc.sync.dma_start(out=w_raw[c][:, i * nb * K:(i + 1) * nb * K].rearrange("p (b k) -> p b k", k=K),
+                              in_=src[:, i * nb:(i + 1) * nb, :])
 
         def load_x(i):
             nc.sync.dma_start(out=x_raw[:, i * 2048:(i + 1) * 2048], in_=x_src[:, i * 2048:(i + 1) * 2048])
@@ -109,10 +110,10 @@ def tile_binarydense_kernel(tc, inputs, weight, bias, nmk, kk, out):
             wg = wg_t[c]
             tp = ps_t.tile([P, 512], F32, name="tp", tag="tp")
             for m in range(4):
-                col = 512 * (2 * bh + m // 2) + 256 * g + 128 * (m % 2)
+                col = 512 * (2 * bh + m % 2) + 256 * g + 128 * (m // 2)
                 nc.tensor.transpose(tp[:, 128 * m:128 * m + 128], wf[:, col:col + 128], ident_f[:])
-            src = tp[:].bitcast(BF16).rearrange("p (m n e) -> p n m e", m=4, n=P, e=2)
-            dst = wg[:, g, :].rearrange("p (n h m e) -> p n h m e", n=P, h=2, m=4, e=2)[:, :, bh, :, :]
+            src = tp[:].bitcast(BF16).rearrange("p (u j e) -> p j u e", u=2, j=2 * P, e=2)
+            dst = wg[:, g, 1024 * bh:1024 * bh + 1024].rearrange("p (j u e) -> p j u e", j=2 * P, u=2, e=2)
             nc.scalar.activation(out=dst, in_=src, func=ACT.Tanh, scale=kk_eff[:, 0:1])
 
         def w_new(c):

from contextlib import ExitStack

import concourse.mybir as mybir
from concourse.masks import make_identity

F32 = mybir.dt.float32
BF16 = mybir.dt.bfloat16
U32 = mybir.dt.uint32
U8 = mybir.dt.uint8
I32 = mybir.dt.int32
FP8X4 = mybir.dt.float8_e4m3fn_x4
ACT = mybir.ActivationFunctionType
ALU = mybir.AluOpType

P = 128
T, K, N = 1024, 1024, 4096
FLOPS = 2 * T * K * N
NA = T // P
CH = 512
NCH = N // CH
G = K // 512
BIG = 3.4e38
KK_THRESHOLD = 1.0e6
PIN = True
A_ST = 2
OFFLOAD = []
QH = (2, 5)
QH0 = (5, 7)
T1_AFTER = 1


def tile_binarydense_kernel(tc, inputs, weight, bias, nmk, kk, out):
    nc = tc.nc
    with ExitStack() as ctx:
        const = ctx.enter_context(tc.tile_pool(name="const", bufs=1))
        wgp = ctx.enter_context(tc.tile_pool(name="wgp", bufs=2))
        wcp = ctx.enter_context(tc.tile_pool(name="wcp", bufs=3))
        osp = ctx.enter_context(tc.tile_pool(name="osp", bufs=12))
        ps_t = ctx.enter_context(tc.psum_pool(name="ps_t", bufs=4))
        ps_a = ctx.enter_context(tc.psum_pool(name="ps_a", bufs=4))
        if PIN:
            ctx.enter_context(tc.manual_schedule())

        kk_bf = const.tile([P, 1], BF16, name="kk_bf")
        nc.sync.dma_start(out=kk_bf[:], in_=kk.partition_broadcast(P))
        nmk_bf = const.tile([P, 1], BF16, name="nmk_bf")
        nc.scalar.dma_start(out=nmk_bf[:], in_=nmk.partition_broadcast(P))
        brow = const.tile([P, CH], BF16, name="brow")
        nc.vector.memset(brow[:].bitcast(I32), 0)
        nc.scalar.dma_start(out=brow[0:NCH, :], in_=bias.rearrange("(c j) -> c j", c=NCH))

        w_raw = []
        for c in range(NCH):
            w_raw.append(const.tile([P, 4 * K], BF16, name="w_raw%d" % c))
        x_raw = const.tile([P, NA * K], BF16, name="x_raw")
        x_src = inputs.rearrange("(p a) k -> p (a k)", a=NA)

        def load_w(c, i, parts):
            src = weight[c * CH:(c + 1) * CH, :].rearrange("(b p) k -> p b k", p=P)
            nb = 4 // parts
            nc.sync.dma_start(out=w_raw[c][:, i * nb * K:(i + 1) * nb * K].rearrange("p (b k) -> p b k", k=K),
                              in_=src[:, i * nb:(i + 1) * nb, :])

        def load_x(i):
            nc.sync.dma_start(out=x_raw[:, i * 2048:(i + 1) * 2048], in_=x_src[:, i * 2048:(i + 1) * 2048])

        load_w(0, 0, 2)
        load_x(0)
        load_w(0, 1, 2)
        load_x(1)
        load_x(2)
        load_x(3)
        for c in range(1, NCH):
            load_w(c, 0, 1)

        ident_f = const.tile([P, P], F32, name="ident_f")
        make_identity(nc, ident_f[:])
        ident_b = const.tile([P, P], BF16, name="ident_b")
        make_identity(nc, ident_b[:])
        kk_m = const.tile([P, 1], F32, name="kk_m")
        nc.vector.tensor_scalar(out=kk_m[:], in0=kk_bf[:], scalar1=KK_THRESHOLD, scalar2=BIG,
                                op0=ALU.is_ge, op1=ALU.mult)
        kk_eff = const.tile([P, 1], F32, name="kk_eff")
        nc.vector.tensor_scalar(out=kk_eff[:], in0=kk_bf[:], scalar1=kk_m[:, 0:1], scalar2=BIG,
                                op0=ALU.add, op1=ALU.min)
        nmk_f = const.tile([P, 1], F32, name="nmk_f")
        nc.vector.tensor_copy(out=nmk_f[:], in_=nmk_bf[:])

        bias_n = const.tile([P, N], F32, name="bias_n")
        xg = const.tile([P, G, NA * 512], BF16, name="xg", align_bytes=64)
        xc = const.tile([P, G, T], U32, name="xc", align_bytes=64)
        xs = const.tile([P, G, T], U8, name="xs", align_bytes=64)
        xgf = xg[:].bitcast(F32)
        xf = x_raw[:].bitcast(F32)
        out_v = out.rearrange("(r a) n -> r a n", a=NA)

        wg_t = {}
        wc_t = {}
        ws_t = {}

        def bias_chunk(c):
            bp = ps_t.tile([P, CH], F32, name="bp", tag="tp")
            nc.tensor.matmul(out=bp[:], lhsT=ident_b[:, c:c + 1].to_broadcast([P, P]), rhs=brow[:],
                             start=True, stop=True)
            nc.scalar.activation(out=bias_n[:, c * CH:(c + 1) * CH], in_=bp[:], func=ACT.Copy,
                                 scale=nmk_f[:, 0:1])

        def w_bank(c, g, bh):
            wf = w_raw[c][:].bitcast(F32)
            wg = wg_t[c]
            tp = ps_t.tile([P, 512], F32, name="tp", tag="tp")
            for m in range(4):
                col = 512 * (2 * bh + m % 2) + 256 * g + 128 * (m // 2)
                nc.tensor.transpose(tp[:, 128 * m:128 * m + 128], wf[:, col:col + 128], ident_f[:])
            src = tp[:].bitcast(BF16).rearrange("p (u j e) -> p j u e", u=2, j=2 * P, e=2)
            dst = wg[:, g, 1024 * bh:1024 * bh + 1024].rearrange("p (j u e) -> p j u e", j=2 * P, u=2, e=2)
            nc.scalar.activation(out=dst, in_=src, func=ACT.Tanh, scale=kk_eff[:, 0:1])

        def w_new(c):
            wg_t[c] = wgp.tile([P, G, 4 * CH], BF16, name="wg", align_bytes=64)

        def w_transpose(c):
            w_new(c)
            for g in range(G):
                for bh in range(2):
                    w_bank(c, g, bh)

        def w_quant(c, g):
            if g == 0:
                wc_t[c] = wcp.tile([P, G, CH], U32, name="wc", align_bytes=64)
                ws_t[c] = wcp.tile([P, G, CH], U8, name="ws", align_bytes=64)
            nc.vector.quantize_mx(out=wc_t[c][:, g, :].bitcast(FP8X4), scales=ws_t[c][:, g, :],
                                  in_=wg_t[c][:, g, :])

        def x_transpose(a, eng):
            tpx = ps_a.tile([P, 512], F32, name="tpx", tag="acc")
            for j in range(4):
                col = 512 * a + 128 * j
                nc.tensor.transpose(tpx[:, 128 * j:128 * j + 128], xf[:, col:col + 128], ident_f[:])
            dst = xgf[:, :, 256 * a:256 * a + 256].rearrange("p g (r u) -> p g r u", u=2)
            src = tpx[:].rearrange("p (g u r) -> p g r u", g=G, u=2)
            if eng == "v":
                nc.vector.tensor_copy(out=dst, in_=src)
            else:
                nc.scalar.copy(out=dst, in_=src)

        def x_quant(q):
            for g in range(G):
                nc.vector.quantize_mx(out=xc[:, g, 256 * q:256 * q + 256].bitcast(FP8X4),
                                      scales=xs[:, g, 256 * q:256 * q + 256],
                                      in_=xg[:, g, 1024 * q:1024 * q + 1024])

        ost_t = {}

        def mx_chunk(c, t_hooks, v_hooks):
            wc = wc_t[c]
            ws = ws_t[c]
            cs = slice(c * CH, (c + 1) * CH)
            for a in range(NA):
                acc = ps_a.tile([P, CH], F32, name="acc", tag="acc")
                for g in range(G):
                    nc.tensor.matmul_mx(out=acc[:],
                                        lhsT=xc[:, g, P * a:P * a + P].bitcast(FP8X4),
                                        lhsT_scale=xs[:, g, P * a:P * a + P],
                                        rhs=wc[:, g, :].bitcast(FP8X4),
                                        rhs_scale=ws[:, g, :],
                                        start=(g == 0), stop=(g == G - 1))
                for f in t_hooks.get(a, []):
                    f()
                if a % A_ST == 0:
                    ost_t[0] = osp.tile([P, A_ST, CH], F32, name="ost")
                ost = ost_t[0]
                if a in OFFLOAD and c < NCH - 1:
                    nc.scalar.activation(out=ost[:, a % A_ST, :], in_=acc[:], func=ACT.Copy,
                                         scale=nmk_f[:, 0:1])
                    nc.gpsimd.tensor_tensor(out=ost[:, a % A_ST, :], in0=ost[:, a % A_ST, :],
                                            in1=bias_n[:, cs], op=ALU.add)
                else:
                    nc.vector.scalar_tensor_tensor(out=ost[:, a % A_ST, :], in0=acc[:], scalar=nmk_f[:, 0:1],
                                                   in1=bias_n[:, cs], op0=ALU.mult, op1=ALU.add)
                if a % A_ST == A_ST - 1:
                    nc.sync.dma_start(out=out_v[:, a - A_ST + 1:a + 1, cs], in_=ost[:])
                for f in v_hooks.get(a, []):
                    f()

        w_new(0)
        w_bank(0, 0, 0)
        w_bank(0, 1, 0)
        x_transpose(0, "v")
        x_transpose(1, "v")
        x_quant(0)
        w_bank(0, 0, 1)
        w_bank(0, 1, 1)
        bias_chunk(0)
        x_transpose(2, "v")
        x_transpose(3, "v")
        x_quant(1)
        for a in range(4, NA):
            x_transpose(a, "s")
        w_quant(0, 0)
        w_quant(0, 1)
        x_quant(2)

        def t_run(c):
            bias_chunk(c)
            w_transpose(c)

        for c in range(NCH):
            t_hooks = {}
            v_hooks = {}
            if c == 0:
                t_hooks[T1_AFTER] = [lambda: t_run(1)]
                v_hooks[0] = [lambda: x_quant(3)]
                v_hooks[QH0[0]] = [lambda: w_quant(1, 0)]
                v_hooks[QH0[1]] = [lambda: w_quant(1, 1)]
            elif c + 1 < NCH:
                n = c + 1
                v_hooks[QH[0]] = [lambda: w_quant(n, 0)]
                v_hooks[QH[1]] = [lambda: w_quant(n, 1)]
                t_run(n)
            mx_chunk(c, t_hooks, v_hooks)
